import numpy as np
import ml_dtypes


def mxq(x, axis, fmt="e4m3"):
    dtype, down = {"e4m3": (ml_dtypes.float8_e4m3fn, 7), "e5m2": (ml_dtypes.float8_e5m2, 14)}[fmt]
    v = np.moveaxis(np.asarray(x, np.float32).astype(ml_dtypes.bfloat16).astype(np.float64), axis, -1)
    blocks = v.reshape(v.shape[:-1] + (-1, 32))
    amax = np.abs(blocks).max(-1, keepdims=True)
    byte = np.maximum(np.where(amax > 0, np.frexp(amax)[1] - 1 + 127, 0) - down, 1)
    scale = np.exp2(byte - 127.0)
    codes = (blocks / scale).astype(np.float32).astype(dtype).astype(np.float64)
    return np.moveaxis((codes * scale).reshape(v.shape), -1, axis)


WIDE = False


def mx_kscale(k):
    if not WIDE:
        return np.ones(k)
    levels = np.array([10, -10, 5, -5, 0])
    if k % 512:
        return np.exp2(np.random.permutation(np.resize(levels, k // 32))).repeat(32)
    a = np.empty((k // 512, 16))
    for p in range(k // 512):
        a[p, :8] = np.random.permutation(np.resize(levels, 8))
        for g in range(8):
            far = levels[np.abs(levels - a[p, g]) >= 10]
            a[p, g + 8] = far[np.random.randint(len(far))]
    return np.exp2(a.ravel()).repeat(32)


BF16 = ml_dtypes.bfloat16


def bf(x):
    return np.asarray(x, np.float32).astype(BF16)


def f64(x):
    return np.asarray(x).astype(np.float64)


B, H, W, NB, BS, F = 1, 16, 32, 8, 512, 512
C = NB * BS
SPARSITY = 0.01


def blockmm(a, w):
    r = np.moveaxis(a, 3, 0).reshape(NB, B * H * W, -1) @ w
    return np.moveaxis(r, 0, 1).reshape(B, H, W, NB, -1)


def setup_inputs():
    s = mx_kscale(F)
    return {"o1k": bf(np.maximum(np.random.standard_normal((B, H, W, NB, F)), 0.0) * 0.27 * s),
            "o1n": bf(np.maximum(np.random.standard_normal((B, H, W, NB, F)), 0.0) * 0.27 * s),
            "w2": bf(np.random.standard_normal((2, NB, F, BS)) * 0.7 / np.sqrt(F) / s[:, None] * s),
            "b2": bf(np.random.standard_normal((2, NB, BS)) * 0.05 * s)}


def reference(o1k, o1n, w2, b2):
    w2, b2 = f64(w2), f64(b2)
    o1kq = mxq(f64(o1k), 4, "e4m3")
    o1nq = mxq(f64(o1n), 4, "e4m3")
    w2a = mxq(w2[0] + w2[1], 1, "e4m3")
    w2b = mxq(w2[0] - w2[1], 1, "e4m3")
    o2k = 0.5 * (blockmm(o1kq, w2a) + blockmm(o1nq, w2b)) + b2[0]
    o2n = 0.5 * (blockmm(o1nq, w2a) + blockmm(mxq(o2k, 4, "e4m3"), w2b)) + b2[1]
    y = (o2k + o2n).reshape(B, H, W, C)
    return np.sign(y) * np.maximum(np.abs(y) - SPARSITY, 0.0)

@@ -1,0 +1,318 @@
+from contextlib import ExitStack
+
+import concourse.mybir as mybir
+from concourse.masks import make_identity
+
+F32 = mybir.dt.float32
+BF16 = mybir.dt.bfloat16
+I32 = mybir.dt.int32
+U32 = mybir.dt.uint32
+U8 = mybir.dt.uint8
+FP8X4 = mybir.dt.float8_e4m3fn_x4
+ALU = mybir.AluOpType
+ACT = mybir.ActivationFunctionType
+
+P = 128
+NB = 8
+T = 512
+F = 512
+TC = T // P
+LAM = 0.01
+FLOPS = 4 * NB * 2 * T * F * F
+VECTOR_REGROUPS = (0,)
+
+
+def tile_afno2d_pb_kernel(tc, o1k, o1n, w2, b2, out):
+    nc = tc.nc
+    x_d = (
+        o1k.rearrange("b h w n f -> (b h w) n f"),
+        o1n.rearrange("b h w n f -> (b h w) n f"),
+    )
+    out_d = out.rearrange("b h w (n o) -> (b h w) n o", n=NB)
+
+    with ExitStack() as ctx:
+        consts = ctx.enter_context(tc.tile_pool(name="consts", bufs=1))
+        loads = ctx.enter_context(tc.tile_pool(name="loads", bufs=3))
+        work = ctx.enter_context(tc.tile_pool(name="work", bufs=2))
+        codes = ctx.enter_context(tc.tile_pool(name="codes", bufs=3))
+        ypool = ctx.enter_context(tc.tile_pool(name="ypool", bufs=2))
+        ps_t = ctx.enter_context(tc.psum_pool(name="ps_t", bufs=2))
+        ps_s = ctx.enter_context(tc.psum_pool(name="ps_s", bufs=2))
+        ps_y = ctx.enter_context(tc.psum_pool(name="ps_y", bufs=4))
+
+        st = {}
+
+        def ok(b):
+            return 0 <= b < NB
+
+        ident = consts.tile([P, P], F32, name="ident")
+        make_identity(nc, ident[:])
+        ones = consts.tile([P, P], BF16, name="ones")
+        nc.vector.memset(ones[:], 1.0)
+        brow = consts.tile([P, NB * F], BF16, name="brow")
+        nc.vector.memset(brow[:].bitcast(I32), 0)
+        nc.sync.dma_start(out=brow[0:2, :], in_=b2.rearrange("i n o -> i (n o)"))
+        btile = consts.tile([P, F], BF16, name="btile")
+        nc.vector.memset(btile[:].bitcast(I32), 0)
+        nc.sync.dma_start(
+            out=btile[0:NB, :],
+            in_=b2[0, :, :],
+        )
+
+        def load_w(b):
+            if not ok(b):
+                return
+            for i in range(2):
+                w = loads.tile([P, 4 * F], BF16, name="w%d" % i)
+                nc.sync.dma_start(
+                    out=w[:],
+                    in_=w2[i, b, :, :].rearrange("(p t) o -> p (t o)", t=4),
+                )
+                st["w", i, b] = w
+
+        def load_x(b):
+            if not ok(b):
+                return
+            for i in range(2):
+                x = loads.tile([P, TC * F], BF16, name="x%d" % i)
+                nc.sync.dma_start(
+                    out=x[:].rearrange("p (c f) -> p c f", c=TC),
+                    in_=x_d[i][:, b, :].rearrange("(c p) f -> p c f", p=P),
+                )
+                st["x", i, b] = x
+
+        pbt = ps_t.tile([P, 4 * P], F32, name="pt")
+        for u in range(2):
+            nc.tensor.transpose(
+                out=pbt[:, u * P : (u + 1) * P], in_=btile[:].bitcast(F32)[:, u : 2 * P : 2], identity=ident[:]
+            )
+        bsb = consts.tile([P, 2 * NB], F32, name="bsb")
+        nc.vector.tensor_copy(
+            out=bsb[:].rearrange("p (n u) -> p n u", u=2),
+            in_=pbt[:, 0 : 2 * P].rearrange("p (u r) -> p r u", u=2)[:, 0:NB, :],
+        )
+        bias0 = consts.tile([P, 4 * NB], F32, name="bias0")
+        nc.vector.tensor_copy(out=bias0[:], in_=bsb[:].bitcast(BF16))
+        bias_y = consts.tile([P, NB * F], F32, name="bias_y")
+        for n in range(NB):
+            pb = ps_y.tile([P, F], F32, name="py")
+            nc.tensor.matmul(
+                out=pb[:], lhsT=ones[:], rhs=brow[:, n * F : (n + 1) * F], start=True, stop=True
+            )
+            if n % 2 == 0:
+                nc.scalar.activation(
+                    out=bias_y[:, n * F : (n + 1) * F], in_=pb[:], func=ACT.Identity, bias=-LAM, scale=1.0
+                )
+            else:
+                nc.vector.tensor_scalar_add(out=bias_y[:, n * F : (n + 1) * F], in0=pb[:], scalar1=-LAM)
+
+        def add_sub(b, which):
+            if not ok(b):
+                return
+            r = work.tile([P, 4 * F], BF16, name="wr%d" % which)
+            nc.vector.tensor_tensor(
+                out=r[:],
+                in0=st["w", 0, b][:],
+                in1=st["w", 1, b][:],
+                op=(ALU.add if which == 0 else ALU.subtract),
+            )
+            st["wr", which, b] = r
+
+        def regroup_w(b, which, e, engine):
+            on_vector = b in VECTOR_REGROUPS or (which == 1 and e == 1)
+            if not ok(b) or (engine == "v") != on_vector:
+                return
+            if ("wg", b) not in st:
+                st["wg", b] = work.tile([P, 8 * F], BF16, name="wg", align_bytes=64)
+            g = st["wg", b][:, which * 4 * F : (which + 1) * 4 * F]
+            dst = g.rearrange("p (e s c i t) -> p e s c t i", e=2, s=2, i=4, t=4)[:, e]
+            src = st["wr", which, b][:].rearrange("p (t c i e s) -> p e s c t i", t=4, i=4, e=2, s=2)[:, e]
+            if engine == "v":
+                nc.vector.tensor_copy(out=dst, in_=src)
+            else:
+                nc.scalar.copy(out=dst, in_=src)
+
+        def transposes(b, i):
+            if not ok(b):
+                return
+            xw = st["x", i, b][:].bitcast(F32)
+            for h in range(2):
+                pt = ps_t.tile([P, 4 * P], F32, name="pt")
+                for cl in range(2):
+                    for u in range(2):
+                        c = 2 * h + cl
+                        nc.tensor.transpose(
+                            out=pt[:, (2 * cl + u) * P : (2 * cl + u + 1) * P],
+                            in_=xw[:, c * 256 + u : (c + 1) * 256 : 2],
+                            identity=ident[:],
+                        )
+                st["pt", i, h, b] = pt
+
+        def evac_x(b, i):
+            if not ok(b):
+                return
+            if i == 0:
+                st["xg", b] = work.tile([P, 8 * T], BF16, name="xg", align_bytes=64)
+            gw = st["xg", b][:].bitcast(F32)
+            for h in range(2):
+                lo = i * 1024 + h * 512
+                nc.scalar.copy(
+                    out=gw[:, lo : lo + 512].rearrange("p (c t u) -> p c t u", c=2, u=2),
+                    in_=st["pt", i, h, b][:].rearrange("p (c u t) -> p c t u", c=2, u=2),
+                )
+
+        def quantise(src, tag, width):
+            c = codes.tile([P, width], U32, name=tag + "c", align_bytes=64)
+            s = codes.tile([P, width], U8, name=tag + "s", align_bytes=64)
+            nc.vector.quantize_mx(out=c[:].bitcast(FP8X4), scales=s[:], in_=src[:])
+            return (c, s)
+
+        def quantise_xw(b):
+            if not ok(b):
+                return
+            st["qx", b] = quantise(st["xg", b], "x", 2 * T)
+            st["qw", b] = quantise(st["wg", b], "w", 2 * F)
+
+        def mx(acc, a, a_lo, b_, b_lo, start, stop):
+            nc.tensor.matmul_mx(
+                out=acc[:],
+                lhsT=a[0][:, a_lo : a_lo + P].bitcast(FP8X4),
+                lhsT_scale=a[1][:, a_lo : a_lo + P],
+                rhs=b_[0][:, b_lo : b_lo + 512].bitcast(FP8X4),
+                rhs_scale=b_[1][:, b_lo : b_lo + 512],
+                start=start,
+                stop=stop,
+            )
+
+        def stage1(b, chunks):
+            if not ok(b):
+                return
+            qx, qw = st["qx", b], st["qw", b]
+            for c in chunks:
+                ps1 = ps_s.tile([P, T], F32, name="ps1")
+                mx(ps1, qw, c * P, qx, 0, True, False)
+                mx(ps1, qw, F + c * P, qx, T, False, True)
+                st["ps1", c, b] = ps1
+
+        def evac1(b, chunks):
+            if not ok(b):
+                return
+            if chunks[0] == 0:
+                st["o2b", b] = work.tile([P, 4 * T], BF16, name="o2b")
+            for c in chunks:
+                nc.scalar.activation(
+                    out=st["o2b", b][:, c * T : (c + 1) * T],
+                    in_=st["ps1", c, b][:],
+                    func=ACT.Identity,
+                    bias=bias0[:, b * 4 + c : b * 4 + c + 1],
+                    scale=0.5,
+                )
+
+        def regroup_o2(b):
+            if not ok(b):
+                return
+            o2g = work.tile([P, 4 * T], BF16, name="o2g", align_bytes=64)
+            nc.vector.tensor_copy(
+                out=o2g[:].rearrange("p (c i j) -> p c j i", i=4, j=4),
+                in_=st["o2b", b][:].rearrange("p (j c i) -> p c j i", i=4, j=4),
+            )
+            st["o2g", b] = o2g
+
+        def quantise_o2(b):
+            if not ok(b):
+                return
+            st["qo", b] = quantise(st["o2g", b], "o", T)
+
+        def y_first(b):
+            if not ok(b):
+                return
+            qx, qw = st["qx", b], st["qw", b]
+            for c in range(TC):
+                py = ps_y.tile([P, F], F32, name="py")
+                mx(py, qx, c * P, qw, 0, True, False)
+                mx(py, qx, T + c * P, qw, F, False, False)
+                mx(py, qx, T + c * P, qw, 0, False, False)
+                st["py", c, b] = py
+
+        def y_last(b):
+            if not ok(b):
+                return
+            for c in range(TC):
+                mx(st["py", c, b], st["qo", b], c * P, st["qw", b], F, False, True)
+
+        def y_bias(b):
+            if not ok(b):
+                return
+            za = ypool.tile([P, TC * F], F32, name="za")
+            for c in range(TC):
+                nc.vector.scalar_tensor_tensor(
+                    out=za[:, c * F : (c + 1) * F].rearrange("p (m t) -> p m t", t=4),
+                    in0=st["py", c, b][:].rearrange("p (t m) -> p m t", t=4),
+                    scalar=0.5,
+                    in1=bias_y[:, b * F : (b + 1) * F].rearrange("p (m t) -> p m t", t=4),
+                    op0=ALU.mult,
+                    op1=ALU.add,
+                )
+            st["za", b] = za
+
+        def y_pieces(b, h):
+            n = 2 if b == NB - 1 else 1
+            w = 2 // n
+            return [
+                (slice((2 * h + k * w) * F, (2 * h + (k + 1) * w) * F), slice((2 * h + k * w) * P, (2 * h + (k + 1) * w) * P))
+                for k in range(n)
+            ]
+
+        def y_neg(b, h):
+            if not ok(b):
+                return
+            if h == 0:
+                st["r2", b] = ypool.tile([P, TC * F], F32, name="r2")
+            for sl, rows in y_pieces(b, h):
+                nc.scalar.activation(
+                    out=st["r2", b][:, sl], in_=st["za", b][:, sl], func=ACT.Relu, bias=-2.0 * LAM, scale=-1.0
+                )
+
+        def y_out(b, h):
+            if not ok(b):
+                return
+            r2 = st["r2", b]
+            for sl, rows in y_pieces(b, h):
+                nc.vector.scalar_tensor_tensor(
+                    out=r2[:, sl], in0=st["za", b][:, sl], scalar=0.0, in1=r2[:, sl], op0=ALU.max, op1=ALU.subtract
+                )
+                nc.sync.dma_start(
+                    out=out_d[rows, b, :].rearrange("(c p) o -> p c o", p=P),
+                    in_=r2[:, sl].rearrange("p (c o) -> p c o", o=F),
+                )
+
+        for i in range(-4, NB + 1):
+            load_x(i + 3)
+            load_w(i + 4)
+            transposes(i + 2, 0)
+            evac1(i, (0, 1))
+            stage1(i, (2, 3))
+            quantise_xw(i + 1)
+            regroup_w(i + 2, 0, 0, "s")
+            y_neg(i - 1, 0)
+            y_out(i - 1, 0)
+            evac1(i, (2, 3))
+            y_first(i)
+            regroup_o2(i)
+            evac_x(i + 2, 0)
+            transposes(i + 2, 1)
+            stage1(i + 1, (0, 1))
+            add_sub(i + 3, 0)
+            quantise_o2(i)
+            y_neg(i - 1, 1)
+            y_out(i - 1, 1)
+            y_last(i)
+            regroup_w(i + 2, 0, 1, "s")
+            regroup_w(i + 2, 1, 0, "s")
+            regroup_w(i + 2, 1, 1, "s")
+            add_sub(i + 3, 1)
+            for which in range(2):
+                for e in range(2):
+                    regroup_w(i + 3, which, e, "v")
+            evac_x(i + 2, 1)
+            y_bias(i)

@@ -19,7 +19,7 @@ F = 512
 TC = T // P
 LAM = 0.01
 FLOPS = 4 * NB * 2 * T * F * F
-VECTOR_REGROUPS = (0,)
+VECTOR_QUARTERS = (4, 2, 2, 1, 0, 0, 0, 0)
 
 
 def tile_afno2d_pb_kernel(tc, o1k, o1n, w2, b2, out):
@@ -59,16 +59,20 @@ def tile_afno2d_pb_kernel(tc, o1k, o1n, w2, b2, out):
             in_=b2[0, :, :],
         )
 
+        def w_pieces(b):
+            n = 2 if b == 0 else 1
+            return [slice(k * 4 * F // n, (k + 1) * 4 * F // n) for k in range(n)]
+
         def load_w(b):
             if not ok(b):
                 return
             for i in range(2):
-                w = loads.tile([P, 4 * F], BF16, name="w%d" % i)
-                nc.sync.dma_start(
-                    out=w[:],
-                    in_=w2[i, b, :, :].rearrange("(p t) o -> p (t o)", t=4),
-                )
-                st["w", i, b] = w
+                st["w", i, b] = loads.tile([P, 4 * F], BF16, name="w%d" % i)
+            for cols in w_pieces(b):
+                for i in range(2):
+                    nc.sync.dma_start(
+                        out=st["w", i, b][:, cols], in_=w2[i, b, :, :].rearrange("(p t) o -> p (t o)", t=4)[:, cols]
+                    )
 
         def load_x(b):
             if not ok(b):
@@ -87,40 +91,42 @@ def tile_afno2d_pb_kernel(tc, o1k, o1n, w2, b2, out):
                 out=pbt[:, u * P : (u + 1) * P], in_=btile[:].bitcast(F32)[:, u : 2 * P : 2], identity=ident[:]
             )
         bsb = consts.tile([P, 2 * NB], F32, name="bsb")
-        nc.vector.tensor_copy(
+        nc.scalar.copy(
             out=bsb[:].rearrange("p (n u) -> p n u", u=2),
             in_=pbt[:, 0 : 2 * P].rearrange("p (u r) -> p r u", u=2)[:, 0:NB, :],
         )
         bias0 = consts.tile([P, 4 * NB], F32, name="bias0")
-        nc.vector.tensor_copy(out=bias0[:], in_=bsb[:].bitcast(BF16))
+        nc.scalar.copy(out=bias0[:], in_=bsb[:].bitcast(BF16))
         bias_y = consts.tile([P, NB * F], F32, name="bias_y")
-        for n in range(NB):
-            pb = ps_y.tile([P, F], F32, name="py")
-            nc.tensor.matmul(
-                out=pb[:], lhsT=ones[:], rhs=brow[:, n * F : (n + 1) * F], start=True, stop=True
-            )
-            if n % 2 == 0:
+
+        def bias_rows():
+            for n in range(NB):
+                pb = ps_y.tile([P, F], F32, name="py")
+                nc.tensor.matmul(
+                    out=pb[:], lhsT=ones[:], rhs=brow[:, n * F : (n + 1) * F], start=True, stop=True
+                )
                 nc.scalar.activation(
                     out=bias_y[:, n * F : (n + 1) * F], in_=pb[:], func=ACT.Identity, bias=-LAM, scale=1.0
                 )
-            else:
-                nc.vector.tensor_scalar_add(out=bias_y[:, n * F : (n + 1) * F], in0=pb[:], scalar1=-LAM)
 
         def add_sub(b, which):
             if not ok(b):
                 return
             r = work.tile([P, 4 * F], BF16, name="wr%d" % which)
-            nc.vector.tensor_tensor(
-                out=r[:],
-                in0=st["w", 0, b][:],
-                in1=st["w", 1, b][:],
-                op=(ALU.add if which == 0 else ALU.subtract),
-            )
+            for cols in w_pieces(b):
+                nc.vector.tensor_tensor(
+                    out=r[:, cols],
+                    in0=st["w", 0, b][:, cols],
+                    in1=st["w", 1, b][:, cols],
+                    op=(ALU.add if which == 0 else ALU.subtract),
+                )
             st["wr", which, b] = r
 
         def regroup_w(b, which, e, engine):
-            on_vector = b in VECTOR_REGROUPS or (which == 1 and e == 1)
-            if not ok(b) or (engine == "v") != on_vector:
+            if not ok(b):
+                return
+            on_vector = 2 * which + e >= 4 - VECTOR_QUARTERS[b]
+            if (engine == "v") != on_vector:
                 return
             if ("wg", b) not in st:
                 st["wg", b] = work.tile([P, 8 * F], BF16, name="wg", align_bytes=64)
@@ -256,6 +262,8 @@ def tile_afno2d_pb_kernel(tc, o1k, o1n, w2, b2, out):
             st["za", b] = za
 
         def y_pieces(b, h):
+            if b < NB - 2:
+                return [(slice(0, TC * F), slice(0, TC * P))] if h else []
             n = 2 if b == NB - 1 else 1
             w = 2 // n
             return [
@@ -315,4 +323,6 @@ def tile_afno2d_pb_kernel(tc, o1k, o1n, w2, b2, out):
                 for e in range(2):
                     regroup_w(i + 3, which, e, "v")
             evac_x(i + 2, 1)
+            if i == -2:
+                bias_rows()
             y_bias(i)

@@ -295,6 +295,8 @@ def tile_afno2d_pb_kernel(tc, o1k, o1n, w2, b2, out):
                 )
 
         for i in range(-4, NB + 1):
+            if i == 1:
+                ctx.enter_context(tc.manual_schedule(engines={mybir.EngineType.PE}))
             load_x(i + 3)
             load_w(i + 4)
             transposes(i + 2, 0)
@@ -315,6 +317,7 @@ def tile_afno2d_pb_kernel(tc, o1k, o1n, w2, b2, out):
             y_neg(i - 1, 1)
             y_out(i - 1, 1)
             y_last(i)
+            evac_x(i + 2, 1)
             regroup_w(i + 2, 0, 1, "s")
             regroup_w(i + 2, 1, 0, "s")
             regroup_w(i + 2, 1, 1, "s")
@@ -322,7 +325,6 @@ def tile_afno2d_pb_kernel(tc, o1k, o1n, w2, b2, out):
             for which in range(2):
                 for e in range(2):
                     regroup_w(i + 3, which, e, "v")
-            evac_x(i + 2, 1)
             if i == -2:
                 bias_rows()
             y_bias(i)

from contextlib import ExitStack

import concourse.mybir as mybir
from concourse.masks import make_identity

F32 = mybir.dt.float32
BF16 = mybir.dt.bfloat16
I32 = mybir.dt.int32
U32 = mybir.dt.uint32
U8 = mybir.dt.uint8
FP8X4 = mybir.dt.float8_e4m3fn_x4
ALU = mybir.AluOpType
ACT = mybir.ActivationFunctionType

P = 128
NB = 8
T = 512
F = 512
TC = T // P
LAM = 0.01
FLOPS = 4 * NB * 2 * T * F * F
VECTOR_QUARTERS = (4, 2, 2, 1, 0, 0, 0, 0)


def tile_afno2d_pb_kernel(tc, o1k, o1n, w2, b2, out):
    nc = tc.nc
    x_d = (
        o1k.rearrange("b h w n f -> (b h w) n f"),
        o1n.rearrange("b h w n f -> (b h w) n f"),
    )
    out_d = out.rearrange("b h w (n o) -> (b h w) n o", n=NB)

    with ExitStack() as ctx:
        consts = ctx.enter_context(tc.tile_pool(name="consts", bufs=1))
        loads = ctx.enter_context(tc.tile_pool(name="loads", bufs=3))
        work = ctx.enter_context(tc.tile_pool(name="work", bufs=2))
        codes = ctx.enter_context(tc.tile_pool(name="codes", bufs=3))
        ypool = ctx.enter_context(tc.tile_pool(name="ypool", bufs=2))
        ps_t = ctx.enter_context(tc.psum_pool(name="ps_t", bufs=2))
        ps_s = ctx.enter_context(tc.psum_pool(name="ps_s", bufs=2))
        ps_y = ctx.enter_context(tc.psum_pool(name="ps_y", bufs=4))

        st = {}

        def ok(b):
            return 0 <= b < NB

        ident = consts.tile([P, P], F32, name="ident")
        make_identity(nc, ident[:])
        ones = consts.tile([P, P], BF16, name="ones")
        nc.vector.memset(ones[:], 1.0)
        brow = consts.tile([P, NB * F], BF16, name="brow")
        nc.vector.memset(brow[:].bitcast(I32), 0)
        nc.sync.dma_start(out=brow[0:2, :], in_=b2.rearrange("i n o -> i (n o)"))
        btile = consts.tile([P, F], BF16, name="btile")
        nc.vector.memset(btile[:].bitcast(I32), 0)
        nc.sync.dma_start(
            out=btile[0:NB, :],
            in_=b2[0, :, :],
        )

        def w_pieces(b):
            n = 2 if b == 0 else 1
            return [slice(k * 4 * F // n, (k + 1) * 4 * F // n) for k in range(n)]

        def load_w(b):
            if not ok(b):
                return
            for i in range(2):
                st["w", i, b] = loads.tile([P, 4 * F], BF16, name="w%d" % i)
            for cols in w_pieces(b):
                for i in range(2):
                    nc.sync.dma_start(
                        out=st["w", i, b][:, cols], in_=w2[i, b, :, :].rearrange("(p t) o -> p (t o)", t=4)[:, cols]
                    )

        def load_x(b):
            if not ok(b):
                return
            for i in range(2):
                x = loads.tile([P, TC * F], BF16, name="x%d" % i)
                nc.sync.dma_start(
                    out=x[:].rearrange("p (c f) -> p c f", c=TC),
                    in_=x_d[i][:, b, :].rearrange("(c p) f -> p c f", p=P),
                )
                st["x", i, b] = x

        pbt = ps_t.tile([P, 4 * P], F32, name="pt")
        for u in range(2):
            nc.tensor.transpose(
                out=pbt[:, u * P : (u + 1) * P], in_=btile[:].bitcast(F32)[:, u : 2 * P : 2], identity=ident[:]
            )
        bsb = consts.tile([P, 2 * NB], F32, name="bsb")
        nc.scalar.copy(
            out=bsb[:].rearrange("p (n u) -> p n u", u=2),
            in_=pbt[:, 0 : 2 * P].rearrange("p (u r) -> p r u", u=2)[:, 0:NB, :],
        )
        bias0 = consts.tile([P, 4 * NB], F32, name="bias0")
        nc.scalar.copy(out=bias0[:], in_=bsb[:].bitcast(BF16))
        bias_y = consts.tile([P, NB * F], F32, name="bias_y")

        def bias_rows():
            for n in range(NB):
                pb = ps_y.tile([P, F], F32, name="py")
                nc.tensor.matmul(
                    out=pb[:], lhsT=ones[:], rhs=brow[:, n * F : (n + 1) * F], start=True, stop=True
                )
                nc.scalar.activation(
                    out=bias_y[:, n * F : (n + 1) * F], in_=pb[:], func=ACT.Identity, bias=-LAM, scale=1.0
                )

        def add_sub(b, which):
            if not ok(b):
                return
            r = work.tile([P, 4 * F], BF16, name="wr%d" % which)
            for cols in w_pieces(b):
                nc.vector.tensor_tensor(
                    out=r[:, cols],
                    in0=st["w", 0, b][:, cols],
                    in1=st["w", 1, b][:, cols],
                    op=(ALU.add if which == 0 else ALU.subtract),
                )
            st["wr", which, b] = r

        def regroup_w(b, which, e, engine):
            if not ok(b):
                return
            on_vector = 2 * which + e >= 4 - VECTOR_QUARTERS[b]
            if (engine == "v") != on_vector:
                return
            if ("wg", b) not in st:
                st["wg", b] = work.tile([P, 8 * F], BF16, name="wg", align_bytes=64)
            g = st["wg", b][:, which * 4 * F : (which + 1) * 4 * F]
            dst = g.rearrange("p (e s c i t) -> p e s c t i", e=2, s=2, i=4, t=4)[:, e]
            src = st["wr", which, b][:].rearrange("p (t c i e s) -> p e s c t i", t=4, i=4, e=2, s=2)[:, e]
            if engine == "v":
                nc.vector.tensor_copy(out=dst, in_=src)
            else:
                nc.scalar.copy(out=dst, in_=src)

        def transposes(b, i):
            if not ok(b):
                return
            xw = st["x", i, b][:].bitcast(F32)
            for h in range(2):
                pt = ps_t.tile([P, 4 * P], F32, name="pt")
                for cl in range(2):
                    for u in range(2):
                        c = 2 * h + cl
                        nc.tensor.transpose(
                            out=pt[:, (2 * cl + u) * P : (2 * cl + u + 1) * P],
                            in_=xw[:, c * 256 + u : (c + 1) * 256 : 2],
                            identity=ident[:],
                        )
                st["pt", i, h, b] = pt

        def evac_x(b, i):
            if not ok(b):
                return
            if i == 0:
                st["xg", b] = work.tile([P, 8 * T], BF16, name="xg", align_bytes=64)
            gw = st["xg", b][:].bitcast(F32)
            for h in range(2):
                lo = i * 1024 + h * 512
                nc.scalar.copy(
                    out=gw[:, lo : lo + 512].rearrange("p (c t u) -> p c t u", c=2, u=2),
                    in_=st["pt", i, h, b][:].rearrange("p (c u t) -> p c t u", c=2, u=2),
                )

        def quantise(src, tag, width):
            c = codes.tile([P, width], U32, name=tag + "c", align_bytes=64)
            s = codes.tile([P, width], U8, name=tag + "s", align_bytes=64)
            nc.vector.quantize_mx(out=c[:].bitcast(FP8X4), scales=s[:], in_=src[:])
            return (c, s)

        def quantise_xw(b):
            if not ok(b):
                return
            st["qx", b] = quantise(st["xg", b], "x", 2 * T)
            st["qw", b] = quantise(st["wg", b], "w", 2 * F)

        def mx(acc, a, a_lo, b_, b_lo, start, stop):
            nc.tensor.matmul_mx(
                out=acc[:],
                lhsT=a[0][:, a_lo : a_lo + P].bitcast(FP8X4),
                lhsT_scale=a[1][:, a_lo : a_lo + P],
                rhs=b_[0][:, b_lo : b_lo + 512].bitcast(FP8X4),
                rhs_scale=b_[1][:, b_lo : b_lo + 512],
                start=start,
                stop=stop,
            )

        def stage1(b, chunks):
            if not ok(b):
                return
            qx, qw = st["qx", b], st["qw", b]
            for c in chunks:
                ps1 = ps_s.tile([P, T], F32, name="ps1")
                mx(ps1, qw, c * P, qx, 0, True, False)
                mx(ps1, qw, F + c * P, qx, T, False, True)
                st["ps1", c, b] = ps1

        def evac1(b, chunks):
            if not ok(b):
                return
            if chunks[0] == 0:
                st["o2b", b] = work.tile([P, 4 * T], BF16, name="o2b")
            for c in chunks:
                nc.scalar.activation(
                    out=st["o2b", b][:, c * T : (c + 1) * T],
                    in_=st["ps1", c, b][:],
                    func=ACT.Identity,
                    bias=bias0[:, b * 4 + c : b * 4 + c + 1],
                    scale=0.5,
                )

        def regroup_o2(b):
            if not ok(b):
                return
            o2g = work.tile([P, 4 * T], BF16, name="o2g", align_bytes=64)
            nc.vector.tensor_copy(
                out=o2g[:].rearrange("p (c i j) -> p c j i", i=4, j=4),
                in_=st["o2b", b][:].rearrange("p (j c i) -> p c j i", i=4, j=4),
            )
            st["o2g", b] = o2g

        def quantise_o2(b):
            if not ok(b):
                return
            st["qo", b] = quantise(st["o2g", b], "o", T)

        def y_first(b):
            if not ok(b):
                return
            qx, qw = st["qx", b], st["qw", b]
            for c in range(TC):
                py = ps_y.tile([P, F], F32, name="py")
                mx(py, qx, c * P, qw, 0, True, False)
                mx(py, qx, T + c * P, qw, F, False, False)
                mx(py, qx, T + c * P, qw, 0, False, False)
                st["py", c, b] = py

        def y_last(b):
            if not ok(b):
                return
            for c in range(TC):
                mx(st["py", c, b], st["qo", b], c * P, st["qw", b], F, False, True)

        def y_bias(b):
            if not ok(b):
                return
            za = ypool.tile([P, TC * F], F32, name="za")
            for c in range(TC):
                nc.vector.scalar_tensor_tensor(
                    out=za[:, c * F : (c + 1) * F].rearrange("p (m t) -> p m t", t=4),
                    in0=st["py", c, b][:].rearrange("p (t m) -> p m t", t=4),
                    scalar=0.5,
                    in1=bias_y[:, b * F : (b + 1) * F].rearrange("p (m t) -> p m t", t=4),
                    op0=ALU.mult,
                    op1=ALU.add,
                )
            st["za", b] = za

        def y_pieces(b, h):
            if b < NB - 2:
                return [(slice(0, TC * F), slice(0, TC * P))] if h else []
            n = 2 if b == NB - 1 else 1
            w = 2 // n
            return [
                (slice((2 * h + k * w) * F, (2 * h + (k + 1) * w) * F), slice((2 * h + k * w) * P, (2 * h + (k + 1) * w) * P))
                for k in range(n)
            ]

        def y_neg(b, h):
            if not ok(b):
                return
            if h == 0:
                st["r2", b] = ypool.tile([P, TC * F], F32, name="r2")
            for sl, rows in y_pieces(b, h):
                nc.scalar.activation(
                    out=st["r2", b][:, sl], in_=st["za", b][:, sl], func=ACT.Relu, bias=-2.0 * LAM, scale=-1.0
                )

        def y_out(b, h):
            if not ok(b):
                return
            r2 = st["r2", b]
            for sl, rows in y_pieces(b, h):
                nc.vector.scalar_tensor_tensor(
                    out=r2[:, sl], in0=st["za", b][:, sl], scalar=0.0, in1=r2[:, sl], op0=ALU.max, op1=ALU.subtract
                )
                nc.sync.dma_start(
                    out=out_d[rows, b, :].rearrange("(c p) o -> p c o", p=P),
                    in_=r2[:, sl].rearrange("p (c o) -> p c o", o=F),
                )

        for i in range(-4, NB + 1):
            if i == 1:
                ctx.enter_context(tc.manual_schedule(engines={mybir.EngineType.PE}))
            load_x(i + 3)
            load_w(i + 4)
            transposes(i + 2, 0)
            evac1(i, (0, 1))
            stage1(i, (2, 3))
            quantise_xw(i + 1)
            regroup_w(i + 2, 0, 0, "s")
            y_neg(i - 1, 0)
            y_out(i - 1, 0)
            evac1(i, (2, 3))
            y_first(i)
            regroup_o2(i)
            evac_x(i + 2, 0)
            transposes(i + 2, 1)
            stage1(i + 1, (0, 1))
            add_sub(i + 3, 0)
            quantise_o2(i)
            y_neg(i - 1, 1)
            y_out(i - 1, 1)
            y_last(i)
            evac_x(i + 2, 1)
            regroup_w(i + 2, 0, 1, "s")
            regroup_w(i + 2, 1, 0, "s")
            regroup_w(i + 2, 1, 1, "s")
            add_sub(i + 3, 1)
            for which in range(2):
                for e in range(2):
                    regroup_w(i + 3, which, e, "v")
            if i == -2:
                bias_rows()
            y_bias(i)
